import numpy as np
import ml_dtypes


def mxq(x, axis, fmt="e4m3"):
    dtype, down = {"e4m3": (ml_dtypes.float8_e4m3fn, 7), "e5m2": (ml_dtypes.float8_e5m2, 14)}[fmt]
    v = np.moveaxis(np.asarray(x, np.float32).astype(ml_dtypes.bfloat16).astype(np.float64), axis, -1)
    blocks = v.reshape(v.shape[:-1] + (-1, 32))
    amax = np.abs(blocks).max(-1, keepdims=True)
    byte = np.maximum(np.where(amax > 0, np.frexp(amax)[1] - 1 + 127, 0) - down, 1)
    scale = np.exp2(byte - 127.0)
    codes = (blocks / scale).astype(np.float32).astype(dtype).astype(np.float64)
    return np.moveaxis((codes * scale).reshape(v.shape), -1, axis)


WIDE = False


def mx_kscale(k):
    if not WIDE:
        return np.ones(k)
    levels = np.array([10, -10, 5, -5, 0])
    a = np.random.permutation(np.resize(levels, k // 512 * 4)).reshape(k // 512, 4)
    idx = np.arange(k)
    return np.exp2(a[idx // 512, idx % 128 // 32])


BF16 = ml_dtypes.bfloat16


def bf(x):
    return np.asarray(x, np.float32).astype(BF16)


def f64(x):
    return np.asarray(x).astype(np.float64)


E2M1 = np.array([0.0, 0.5, 1.0, 1.5, 2.0, 3.0, 4.0, 6.0, -0.0, -0.5, -1.0, -1.5, -2.0, -3.0, -4.0, -6.0])


def pack_weight(w, fmt):
    k, n = w.shape
    w = f64(bf(w)).reshape(k // 32, 32, n)
    amax = np.abs(w).max(1)
    if fmt == "e4m3":
        byte = np.frexp(amax)[1] - 1 + 127 - 7
    else:
        mant, ex = np.frexp(amax / 6.0)
        byte = np.where(mant > 0.5, ex, ex - 1) + 127
    byte = np.clip(np.where(amax > 0, byte, 1), 1, 254)
    scaled = (w * np.exp2(127.0 - byte)[:, None, :]).reshape(k, n).astype(np.float32)
    by_word = np.ascontiguousarray(scaled.reshape(k // 512, 128, 4, n).transpose(0, 1, 3, 2))
    if fmt == "e4m3":
        words = by_word.astype(ml_dtypes.float8_e4m3fn).view(np.uint8)
    else:
        c = by_word.astype(ml_dtypes.float4_e2m1fn).view(np.uint8) & 0xF
        words = c[..., 0::2] | (c[..., 1::2] << 4)
    return np.ascontiguousarray(words), np.ascontiguousarray(byte.astype(np.uint8).reshape(k // 512, 16, n))


def unpack_weight(words, scales, fmt):
    g, p, n, _ = words.shape
    if fmt == "e4m3":
        vals = np.ascontiguousarray(words).view(ml_dtypes.float8_e4m3fn).astype(np.float64)
    else:
        nib = np.empty((g, p, n, 4), np.uint8)
        nib[..., 0::2] = words & 0xF
        nib[..., 1::2] = words >> 4
        vals = E2M1[nib]
    vals = vals * np.repeat(np.exp2(scales.astype(np.float64) - 127.0), 8, axis=1)[..., None]
    return vals.transpose(0, 1, 3, 2).reshape(g * 512, n)


L, T, F, D = 4, 128, 1536, 512
FMT = "e4m3"


def setup_inputs():
    s, t = mx_kscale(D), mx_kscale(F)
    x = bf(np.random.standard_normal((L, T, D)) * s)
    enc = np.random.standard_normal((L, F, D)) / np.sqrt(D) / s * t[:, None]
    b_enc = bf(np.random.standard_normal((L, F)) * 0.2 * t)
    b_dec = bf(np.random.standard_normal((L, D)) * 0.3)
    dec = np.random.standard_normal((L, L, F, D)) / np.sqrt(F) / t[:, None]
    enc_words, enc_scales = pack_weight(np.ascontiguousarray(enc.swapaxes(1, 2)).reshape(-1, F), FMT)
    dec_words, dec_scales = pack_weight(dec.reshape(-1, D), FMT)
    return {"x": x,
            "W_enc_words": enc_words, "W_enc_scales": enc_scales,
            "b_enc": b_enc,
            "b_dec": b_dec,
            "W_dec_words": dec_words, "W_dec_scales": dec_scales,
            "dec_mask": np.triu(np.ones((L, L), dtype=bool))}


def reference(x, W_enc_words, W_enc_scales, b_enc, b_dec, W_dec_words, W_dec_scales, dec_mask):
    pre = mxq(f64(x), 2, "e4m3") @ unpack_weight(W_enc_words, W_enc_scales, FMT).reshape(L, D, F)
    acts = np.maximum(pre + f64(b_enc)[:, None, :], 0.0)
    aq = mxq(acts, 2, "e4m3")
    Wd = unpack_weight(W_dec_words, W_dec_scales, FMT).reshape(L, L, F, D)
    keep = np.asarray(dec_mask)
    recon = []
    for j in range(L):
        src = np.nonzero(keep[:, j])[0]
        a = np.concatenate([aq[i] for i in src], axis=1)
        w = Wd[src, j].reshape(len(src) * F, D)
        recon.append((a @ w) + f64(b_dec)[j])
    return np.stack(recon)

@@ -1,0 +1,158 @@
+import concourse.mybir as mybir
+from concourse.masks import make_identity
+
+F32 = mybir.dt.float32
+BF16 = mybir.dt.bfloat16
+I32 = mybir.dt.int32
+U8 = mybir.dt.uint8
+FP8X4 = mybir.dt.float8_e4m3fn_x4
+ADD = mybir.AluOpType.add
+
+L, T, F, D = 4, 128, 1536, 512
+P = 128
+PACK = 4
+K_PASS = P * PACK
+FG = F // K_PASS
+QUADRANTS = 4
+PAIRS = L * (L + 1) // 2
+
+FLOPS = 2 * T * D * F * (L + PAIRS)
+BYTES = (
+    2 * L * T * D
+    + (L + PAIRS) * (F * D + F * D // 32)
+    + 2 * L * (F + D)
+    + 4 * L * T * D
+)
+
+
+def tile_crosslayertranscoder_e_kernel(
+    tc, x, W_enc_words, W_enc_scales, b_enc, b_dec, W_dec_words, W_dec_scales, dec_mask, out
+):
+    nc = tc.nc
+    with tc.tile_pool(name="keep", bufs=1) as keep, tc.tile_pool(name="work", bufs=3) as work, tc.psum_pool(
+        name="psum_pre", bufs=2
+    ) as psum_pre, tc.psum_pool(name="psum_tr", bufs=2) as psum_tr, tc.psum_pool(name="psum_acc", bufs=1) as psum_acc:
+        ident_f32 = keep.tile([P, P], F32)
+        make_identity(nc, ident_f32[:])
+        ident_bf16 = keep.tile([P, P], BF16)
+        nc.vector.tensor_copy(out=ident_bf16[:], in_=ident_f32[:])
+
+        enc_planes = keep.tile([P, F], U8, align_bytes=64)
+        dec_planes = keep.tile([P, L * FG, D], U8, align_bytes=64)
+        bias_rows = keep.tile([P, K_PASS], BF16)
+        nc.vector.memset(enc_planes[:].bitcast(I32), 0)
+        nc.vector.memset(bias_rows[:], 0.0)
+        nc.vector.memset(dec_planes[:].rearrange("p s n -> p (s n)").bitcast(I32), 0)
+
+        nc.scalar.dma_start(out=bias_rows[0 : L * FG, :], in_=b_enc.rearrange("l (g k) -> (l g) k", k=K_PASS))
+        nc.scalar.dma_start(out=bias_rows[L * FG : L * FG + L, :], in_=b_dec)
+
+        x_sb = keep.tile([T, L, D], BF16)
+        for l in range(L):
+            nc.sync.dma_start(out=x_sb[:, l, :], in_=x[l])
+        for quadrant in range(QUADRANTS):
+            nc.sync.dma_start(
+                out=enc_planes[32 * quadrant : 32 * quadrant + 4 * L, :].bitcast(I32),
+                in_=W_enc_scales[:, 4 * quadrant : 4 * quadrant + 4, :].bitcast(I32),
+            )
+        enc_words = keep.tile([P, L, F], I32, align_bytes=64)
+        for l in range(L):
+            nc.sync.dma_start(out=enc_words[:, l, :], in_=W_enc_words[l].rearrange("p n t -> p (n t)").bitcast(I32))
+        dec_words = []
+        for i in range(L):
+            slots = (L - i) * FG
+            first = (L * i + i) * FG
+            for r in range(4):
+                nc.sync.dma_start(
+                    out=dec_planes[4 * i + r : P : 32, 0:slots, :].bitcast(I32),
+                    in_=W_dec_scales[first : first + slots, r : 16 : 4, :].rearrange("s q n -> q s n").bitcast(I32),
+                )
+            words = keep.tile([P, slots, D], I32, name="dec_words%d" % i, align_bytes=64)
+            dec_words.append(words)
+            for j in range(i, L):
+                at = (j - i) * FG
+                nc.sync.dma_start(
+                    out=words[:, at : at + FG, :],
+                    in_=W_dec_words[first + at : first + at + FG].rearrange("g p n t -> p g (n t)").bitcast(I32),
+                )
+
+        x_grouped = keep.tile([P, L, T * PACK], BF16, align_bytes=64)
+        x_codes = keep.tile([P, L, T], I32, align_bytes=64)
+        x_planes = keep.tile([P, L, T], U8, align_bytes=64)
+        for l in range(L):
+            x_pairs = x_sb[:, l, :].bitcast(F32)
+            xT = psum_tr.tile([P, 2, T], F32, tag="tr")
+            for u in range(2):
+                nc.tensor.transpose(xT[:, u, :], x_pairs[:, u : D // 2 : 2], ident_f32[:])
+            nc.scalar.copy(
+                out=x_grouped[:, l, :].bitcast(F32).rearrange("p (k u) -> p k u", u=2),
+                in_=xT[:].rearrange("p u k -> p k u"),
+            )
+            nc.vector.quantize_mx(out=x_codes[:, l, :].bitcast(FP8X4), scales=x_planes[:, l, :], in_=x_grouped[:, l, :])
+
+        biasT = psum_tr.tile([P, PACK, P], BF16, tag="tr")
+        for t in range(PACK):
+            nc.tensor.transpose(biasT[:, t, :], bias_rows[:, t:K_PASS:PACK], ident_bf16[:])
+        enc_bias = keep.tile([P, L * FG, PACK], F32)
+        nc.vector.tensor_copy(out=enc_bias[:], in_=biasT[:, :, 0 : L * FG].rearrange("p t r -> p r t"))
+
+        acts_grouped = keep.tile([P, L, FG, T * PACK], BF16, align_bytes=64)
+        acts_codes = keep.tile([P, L, FG, T], I32, align_bytes=64)
+        acts_planes = keep.tile([P, L, FG, T], U8, align_bytes=64)
+        for l in range(L):
+            for g in range(FG):
+                features = slice(g * K_PASS, (g + 1) * K_PASS)
+                pre = psum_pre.tile([T, K_PASS], F32, tag="pre")
+                nc.tensor.matmul_mx(
+                    out=pre[:],
+                    lhsT=x_codes[:, l, :].bitcast(FP8X4),
+                    lhsT_scale=x_planes[:, l, :],
+                    rhs=enc_words[:, l, features].bitcast(FP8X4),
+                    rhs_scale=enc_planes[4 * l : P, features],
+                    start=True,
+                    stop=True,
+                )
+                pre_sorted = work.tile([T, PACK, P], F32)
+                nc.scalar.copy(out=pre_sorted[:], in_=pre[:].rearrange("k (p t) -> k t p", t=PACK))
+                preT = psum_tr.tile([P, PACK, T], F32, tag="tr")
+                for t in range(PACK):
+                    nc.tensor.transpose(preT[:, t, :], pre_sorted[:, t, :], ident_f32[:])
+                grouped = acts_grouped[:, l, g, :]
+                nc.vector.tensor_tensor(
+                    out=grouped.rearrange("p (k t) -> p k t", t=PACK),
+                    in0=preT[:].rearrange("p t k -> p k t"),
+                    in1=enc_bias[:, l * FG + g, :].unsqueeze(1).to_broadcast([P, T, PACK]),
+                    op=ADD,
+                )
+                nc.vector.tensor_scalar_max(out=grouped, in0=grouped, scalar1=0.0)
+                nc.vector.quantize_mx(
+                    out=acts_codes[:, l, g, :].bitcast(FP8X4), scales=acts_planes[:, l, g, :], in_=grouped
+                )
+
+        dec_bias = keep.tile([T, L, D], F32)
+        for j in range(L):
+            spread = psum_pre.tile([T, D], F32, tag="pre")
+            row = L * FG + j
+            nc.tensor.matmul(
+                out=spread[:], lhsT=ident_bf16[:, row : row + 1].to_broadcast([P, T]), rhs=bias_rows[:], start=True, stop=True
+            )
+            nc.scalar.copy(out=dec_bias[:, j, :], in_=spread[:])
+
+        acc = [psum_acc.tile([T, D], F32, name="acc%d" % j) for j in range(L)]
+        for i in range(L):
+            for j in range(i, L):
+                for g in range(FG):
+                    slot = (j - i) * FG + g
+                    nc.tensor.matmul_mx(
+                        out=acc[j][:],
+                        lhsT=acts_codes[:, i, g, :].bitcast(FP8X4),
+                        lhsT_scale=acts_planes[:, i, g, :],
+                        rhs=dec_words[i][:, slot, :].bitcast(FP8X4),
+                        rhs_scale=dec_planes[4 * i : P, slot, :],
+                        start=(i == 0 and g == 0),
+                        stop=(i == j and g == FG - 1),
+                    )
+                if i == j:
+                    recon = work.tile([T, D], F32)
+                    nc.vector.tensor_tensor(out=recon[:], in0=acc[j][:], in1=dec_bias[:, j, :], op=ADD)
+                    nc.scalar.dma_start(out=out[j], in_=recon[:])

@@ -16,6 +16,9 @@ FG = F // K_PASS
 QUADRANTS = 4
 PAIRS = L * (L + 1) // 2
 
+CHUNKS = L * FG
+LAG = 2 * FG
+
 FLOPS = 2 * T * D * F * (L + PAIRS)
 BYTES = (
     2 * L * T * D
@@ -31,11 +34,11 @@ def tile_crosslayertranscoder_e_kernel(
     nc = tc.nc
     with tc.tile_pool(name="keep", bufs=1) as keep, tc.tile_pool(name="work", bufs=3) as work, tc.psum_pool(
         name="psum_pre", bufs=2
-    ) as psum_pre, tc.psum_pool(name="psum_tr", bufs=2) as psum_tr, tc.psum_pool(name="psum_acc", bufs=1) as psum_acc:
+    ) as psum_pre, tc.psum_pool(name="psum_tr", bufs=2) as psum_tr, tc.psum_pool(
+        name="psum_acc", bufs=1
+    ) as psum_acc, tc.manual_schedule():
         ident_f32 = keep.tile([P, P], F32)
         make_identity(nc, ident_f32[:])
-        ident_bf16 = keep.tile([P, P], BF16)
-        nc.vector.tensor_copy(out=ident_bf16[:], in_=ident_f32[:])
 
         enc_planes = keep.tile([P, F], U8, align_bytes=64)
         dec_planes = keep.tile([P, L * FG, D], U8, align_bytes=64)
@@ -43,9 +46,11 @@ def tile_crosslayertranscoder_e_kernel(
         nc.vector.memset(enc_planes[:].bitcast(I32), 0)
         nc.vector.memset(bias_rows[:], 0.0)
         nc.vector.memset(dec_planes[:].rearrange("p s n -> p (s n)").bitcast(I32), 0)
+        ident_bf16 = keep.tile([P, P], BF16)
+        nc.vector.tensor_copy(out=ident_bf16[:], in_=ident_f32[:])
 
-        nc.scalar.dma_start(out=bias_rows[0 : L * FG, :], in_=b_enc.rearrange("l (g k) -> (l g) k", k=K_PASS))
-        nc.scalar.dma_start(out=bias_rows[L * FG : L * FG + L, :], in_=b_dec)
+        nc.scalar.dma_start(out=bias_rows[0:CHUNKS, :], in_=b_enc.rearrange("l (g k) -> (l g) k", k=K_PASS))
+        nc.scalar.dma_start(out=bias_rows[CHUNKS : CHUNKS + L, :], in_=b_dec)
 
         x_sb = keep.tile([T, L, D], BF16)
         for l in range(L):
@@ -93,66 +98,88 @@ def tile_crosslayertranscoder_e_kernel(
         biasT = psum_tr.tile([P, PACK, P], BF16, tag="tr")
         for t in range(PACK):
             nc.tensor.transpose(biasT[:, t, :], bias_rows[:, t:K_PASS:PACK], ident_bf16[:])
-        enc_bias = keep.tile([P, L * FG, PACK], F32)
-        nc.vector.tensor_copy(out=enc_bias[:], in_=biasT[:, :, 0 : L * FG].rearrange("p t r -> p r t"))
-
-        acts_grouped = keep.tile([P, L, FG, T * PACK], BF16, align_bytes=64)
-        acts_codes = keep.tile([P, L, FG, T], I32, align_bytes=64)
-        acts_planes = keep.tile([P, L, FG, T], U8, align_bytes=64)
-        for l in range(L):
-            for g in range(FG):
-                features = slice(g * K_PASS, (g + 1) * K_PASS)
-                pre = psum_pre.tile([T, K_PASS], F32, tag="pre")
-                nc.tensor.matmul_mx(
-                    out=pre[:],
-                    lhsT=x_codes[:, l, :].bitcast(FP8X4),
-                    lhsT_scale=x_planes[:, l, :],
-                    rhs=enc_words[:, l, features].bitcast(FP8X4),
-                    rhs_scale=enc_planes[4 * l : P, features],
-                    start=True,
-                    stop=True,
-                )
-                pre_sorted = work.tile([T, PACK, P], F32)
-                nc.scalar.copy(out=pre_sorted[:], in_=pre[:].rearrange("k (p t) -> k t p", t=PACK))
-                preT = psum_tr.tile([P, PACK, T], F32, tag="tr")
-                for t in range(PACK):
-                    nc.tensor.transpose(preT[:, t, :], pre_sorted[:, t, :], ident_f32[:])
-                grouped = acts_grouped[:, l, g, :]
-                nc.vector.tensor_tensor(
-                    out=grouped.rearrange("p (k t) -> p k t", t=PACK),
-                    in0=preT[:].rearrange("p t k -> p k t"),
-                    in1=enc_bias[:, l * FG + g, :].unsqueeze(1).to_broadcast([P, T, PACK]),
-                    op=ADD,
-                )
-                nc.vector.tensor_scalar_max(out=grouped, in0=grouped, scalar1=0.0)
-                nc.vector.quantize_mx(
-                    out=acts_codes[:, l, g, :].bitcast(FP8X4), scales=acts_planes[:, l, g, :], in_=grouped
-                )
+        enc_bias = keep.tile([P, CHUNKS, PACK], F32)
+        nc.vector.tensor_copy(out=enc_bias[:], in_=biasT[:, :, 0:CHUNKS].rearrange("p t r -> p r t"))
 
         dec_bias = keep.tile([T, L, D], F32)
         for j in range(L):
             spread = psum_pre.tile([T, D], F32, tag="pre")
-            row = L * FG + j
+            row = CHUNKS + j
             nc.tensor.matmul(
                 out=spread[:], lhsT=ident_bf16[:, row : row + 1].to_broadcast([P, T]), rhs=bias_rows[:], start=True, stop=True
             )
             nc.scalar.copy(out=dec_bias[:, j, :], in_=spread[:])
 
+        acts_grouped = keep.tile([P, CHUNKS, T * PACK], BF16, align_bytes=64)
+        acts_codes = keep.tile([P, CHUNKS, T], I32, align_bytes=64)
+        acts_planes = keep.tile([P, CHUNKS, T], U8, align_bytes=64)
+        sorted_sums = {}
+
+        def encoder_pass(chunk):
+            l, g = divmod(chunk, FG)
+            features = slice(g * K_PASS, (g + 1) * K_PASS)
+            pre = psum_pre.tile([T, K_PASS], F32, tag="pre")
+            nc.tensor.matmul_mx(
+                out=pre[:],
+                lhsT=x_codes[:, l, :].bitcast(FP8X4),
+                lhsT_scale=x_planes[:, l, :],
+                rhs=enc_words[:, l, features].bitcast(FP8X4),
+                rhs_scale=enc_planes[4 * l : P, features],
+                start=True,
+                stop=True,
+            )
+            pre_sorted = work.tile([T, PACK, P], F32)
+            nc.scalar.copy(out=pre_sorted[:], in_=pre[:].rearrange("k (p t) -> k t p", t=PACK))
+            sorted_sums[chunk] = pre_sorted
+
+        def encoder_transpose(chunk):
+            preT = psum_tr.tile([P, PACK, T], F32, tag="tr")
+            for t in range(PACK):
+                nc.tensor.transpose(preT[:, t, :], sorted_sums[chunk][:, t, :], ident_f32[:])
+            nc.vector.tensor_tensor(
+                out=acts_grouped[:, chunk, :].rearrange("p (k t) -> p k t", t=PACK),
+                in0=preT[:].rearrange("p t k -> p k t"),
+                in1=enc_bias[:, chunk, :].unsqueeze(1).to_broadcast([P, T, PACK]),
+                op=ADD,
+            )
+
+        def encoder_relu(chunk):
+            nc.vector.tensor_scalar_max(out=acts_grouped[:, chunk, :], in0=acts_grouped[:, chunk, :], scalar1=0.0)
+
+        def encoder_quantise(chunk):
+            nc.vector.quantize_mx(
+                out=acts_codes[:, chunk, :].bitcast(FP8X4), scales=acts_planes[:, chunk, :], in_=acts_grouped[:, chunk, :]
+            )
+
         acc = [psum_acc.tile([T, D], F32, name="acc%d" % j) for j in range(L)]
-        for i in range(L):
-            for j in range(i, L):
-                for g in range(FG):
-                    slot = (j - i) * FG + g
-                    nc.tensor.matmul_mx(
-                        out=acc[j][:],
-                        lhsT=acts_codes[:, i, g, :].bitcast(FP8X4),
-                        lhsT_scale=acts_planes[:, i, g, :],
-                        rhs=dec_words[i][:, slot, :].bitcast(FP8X4),
-                        rhs_scale=dec_planes[4 * i : P, slot, :],
-                        start=(i == 0 and g == 0),
-                        stop=(i == j and g == FG - 1),
-                    )
-                if i == j:
-                    recon = work.tile([T, D], F32)
-                    nc.vector.tensor_tensor(out=recon[:], in0=acc[j][:], in1=dec_bias[:, j, :], op=ADD)
-                    nc.scalar.dma_start(out=out[j], in_=recon[:])
+
+        def decoder_block(i, j):
+            for g in range(FG):
+                slot = (j - i) * FG + g
+                nc.tensor.matmul_mx(
+                    out=acc[j][:],
+                    lhsT=acts_codes[:, i * FG + g, :].bitcast(FP8X4),
+                    lhsT_scale=acts_planes[:, i * FG + g, :],
+                    rhs=dec_words[i][:, slot, :].bitcast(FP8X4),
+                    rhs_scale=dec_planes[4 * i : P, slot, :],
+                    start=(i == 0 and g == 0),
+                    stop=(i == j and g == FG - 1),
+                )
+            if i == j:
+                recon = work.tile([T, D], F32)
+                nc.vector.tensor_tensor(out=recon[:], in0=acc[j][:], in1=dec_bias[:, j, :], op=ADD)
+                nc.sync.dma_start(out=out[j], in_=recon[:])
+
+        blocks = [(i, j) for i in range(L) for j in range(i, L)]
+        encoder_pass(0)
+        for step in range(LAG + PAIRS):
+            if step + 1 < CHUNKS:
+                encoder_pass(step + 1)
+            if step >= LAG:
+                decoder_block(*blocks[step - LAG])
+            if 1 <= step <= CHUNKS:
+                encoder_relu(step - 1)
+            if step < CHUNKS:
+                encoder_transpose(step)
+            if 1 <= step <= CHUNKS:
+                encoder_quantise(step - 1)

@@ -17,7 +17,7 @@ QUADRANTS = 4
 PAIRS = L * (L + 1) // 2
 
 CHUNKS = L * FG
-LAG = 2 * FG
+LAG = 3 * FG
 
 FLOPS = 2 * T * D * F * (L + PAIRS)
 BYTES = (
@@ -63,7 +63,6 @@ def tile_crosslayertranscoder_e_kernel(
         enc_words = keep.tile([P, L, F], I32, align_bytes=64)
         for l in range(L):
             nc.sync.dma_start(out=enc_words[:, l, :], in_=W_enc_words[l].rearrange("p n t -> p (n t)").bitcast(I32))
-        dec_words = []
         for i in range(L):
             slots = (L - i) * FG
             first = (L * i + i) * FG
@@ -72,6 +71,10 @@ def tile_crosslayertranscoder_e_kernel(
                     out=dec_planes[4 * i + r : P : 32, 0:slots, :].bitcast(I32),
                     in_=W_dec_scales[first : first + slots, r : 16 : 4, :].rearrange("s q n -> q s n").bitcast(I32),
                 )
+        dec_words = []
+        for i in range(L):
+            slots = (L - i) * FG
+            first = (L * i + i) * FG
             words = keep.tile([P, slots, D], I32, name="dec_words%d" % i, align_bytes=64)
             dec_words.append(words)
             for j in range(i, L):

@@ -17,7 +17,7 @@ QUADRANTS = 4
 PAIRS = L * (L + 1) // 2
 
 CHUNKS = L * FG
-LAG = 3 * FG
+LAG = 2 * FG
 
 FLOPS = 2 * T * D * F * (L + PAIRS)
 BYTES = (
@@ -26,6 +26,10 @@ BYTES = (
     + 2 * L * (F + D)
     + 4 * L * T * D
 )
+
+
+def first_slot(i):
+    return FG * (i * L - i * (i - 1) // 2)
 
 
 def tile_crosslayertranscoder_e_kernel(
@@ -41,11 +45,13 @@ def tile_crosslayertranscoder_e_kernel(
         make_identity(nc, ident_f32[:])
 
         enc_planes = keep.tile([P, F], U8, align_bytes=64)
-        dec_planes = keep.tile([P, L * FG, D], U8, align_bytes=64)
+        dec_planes = keep.tile([P, PAIRS * FG, D], U8, align_bytes=64)
         bias_rows = keep.tile([P, K_PASS], BF16)
         nc.vector.memset(enc_planes[:].bitcast(I32), 0)
         nc.vector.memset(bias_rows[:], 0.0)
-        nc.vector.memset(dec_planes[:].rearrange("p s n -> p (s n)").bitcast(I32), 0)
+        for i in range(L):
+            layer = dec_planes[:, first_slot(i) : first_slot(i + 1), :]
+            nc.vector.memset(layer.rearrange("p s n -> p (s n)").bitcast(I32), 0)
         ident_bf16 = keep.tile([P, P], BF16)
         nc.vector.tensor_copy(out=ident_bf16[:], in_=ident_f32[:])
 
@@ -63,25 +69,20 @@ def tile_crosslayertranscoder_e_kernel(
         enc_words = keep.tile([P, L, F], I32, align_bytes=64)
         for l in range(L):
             nc.sync.dma_start(out=enc_words[:, l, :], in_=W_enc_words[l].rearrange("p n t -> p (n t)").bitcast(I32))
+        dec_words = keep.tile([P, PAIRS * FG, D], I32, align_bytes=64)
         for i in range(L):
-            slots = (L - i) * FG
-            first = (L * i + i) * FG
+            slot = first_slot(i)
+            group = (L * i + i) * FG
+            count = (L - i) * FG
             for r in range(4):
-                nc.sync.dma_start(
-                    out=dec_planes[4 * i + r : P : 32, 0:slots, :].bitcast(I32),
-                    in_=W_dec_scales[first : first + slots, r : 16 : 4, :].rearrange("s q n -> q s n").bitcast(I32),
+                nc.gpsimd.dma_start(
+                    out=dec_planes[4 * i + r : P : 32, slot : slot + count, :].bitcast(F32),
+                    in_=W_dec_scales[group : group + count, r : 16 : 4, :].rearrange("s q n -> q s n").bitcast(F32),
                 )
-        dec_words = []
-        for i in range(L):
-            slots = (L - i) * FG
-            first = (L * i + i) * FG
-            words = keep.tile([P, slots, D], I32, name="dec_words%d" % i, align_bytes=64)
-            dec_words.append(words)
-            for j in range(i, L):
-                at = (j - i) * FG
+            for at in range(0, count, FG):
                 nc.sync.dma_start(
-                    out=words[:, at : at + FG, :],
-                    in_=W_dec_words[first + at : first + at + FG].rearrange("g p n t -> p g (n t)").bitcast(I32),
+                    out=dec_words[:, slot + at : slot + at + FG, :],
+                    in_=W_dec_words[group + at : group + at + FG].rearrange("g p n t -> p g (n t)").bitcast(I32),
                 )
 
         x_grouped = keep.tile([P, L, T * PACK], BF16, align_bytes=64)
@@ -158,12 +159,12 @@ def tile_crosslayertranscoder_e_kernel(
 
         def decoder_block(i, j):
             for g in range(FG):
-                slot = (j - i) * FG + g
+                slot = first_slot(i) + (j - i) * FG + g
                 nc.tensor.matmul_mx(
                     out=acc[j][:],
                     lhsT=acts_codes[:, i * FG + g, :].bitcast(FP8X4),
                     lhsT_scale=acts_planes[:, i * FG + g, :],
-                    rhs=dec_words[i][:, slot, :].bitcast(FP8X4),
+                    rhs=dec_words[:, slot, :].bitcast(FP8X4),
                     rhs_scale=dec_planes[4 * i : P, slot, :],
                     start=(i == 0 and g == 0),
                     stop=(i == j and g == FG - 1),

@@ -45,13 +45,12 @@ def tile_crosslayertranscoder_e_kernel(
         make_identity(nc, ident_f32[:])
 
         enc_planes = keep.tile([P, F], U8, align_bytes=64)
-        dec_planes = keep.tile([P, PAIRS * FG, D], U8, align_bytes=64)
+        dec_planes = [keep.tile([P, (L - i) * FG, D], U8, name="dec_planes%d" % i, align_bytes=64) for i in range(L)]
         bias_rows = keep.tile([P, K_PASS], BF16)
         nc.vector.memset(enc_planes[:].bitcast(I32), 0)
         nc.vector.memset(bias_rows[:], 0.0)
         for i in range(L):
-            layer = dec_planes[:, first_slot(i) : first_slot(i + 1), :]
-            nc.vector.memset(layer.rearrange("p s n -> p (s n)").bitcast(I32), 0)
+            nc.vector.memset(dec_planes[i][:].rearrange("p s n -> p (s n)").bitcast(I32), 0)
         ident_bf16 = keep.tile([P, P], BF16)
         nc.vector.tensor_copy(out=ident_bf16[:], in_=ident_f32[:])
 
@@ -76,7 +75,7 @@ def tile_crosslayertranscoder_e_kernel(
             count = (L - i) * FG
             for r in range(4):
                 nc.gpsimd.dma_start(
-                    out=dec_planes[4 * i + r : P : 32, slot : slot + count, :].bitcast(F32),
+                    out=dec_planes[i][4 * i + r : P : 32, :, :].bitcast(F32),
                     in_=W_dec_scales[group : group + count, r : 16 : 4, :].rearrange("s q n -> q s n").bitcast(F32),
                 )
             for at in range(0, count, FG):
@@ -159,13 +158,13 @@ def tile_crosslayertranscoder_e_kernel(
 
         def decoder_block(i, j):
             for g in range(FG):
-                slot = first_slot(i) + (j - i) * FG + g
+                at = (j - i) * FG + g
                 nc.tensor.matmul_mx(
                     out=acc[j][:],
                     lhsT=acts_codes[:, i * FG + g, :].bitcast(FP8X4),
                     lhsT_scale=acts_planes[:, i * FG + g, :],
-                    rhs=dec_words[:, slot, :].bitcast(FP8X4),
-                    rhs_scale=dec_planes[4 * i : P, slot, :],
+                    rhs=dec_words[:, first_slot(i) + at, :].bitcast(FP8X4),
+                    rhs_scale=dec_planes[i][4 * i : P, at, :],
                     start=(i == 0 and g == 0),
                     stop=(i == j and g == FG - 1),
                 )

@@ -18,6 +18,9 @@ PAIRS = L * (L + 1) // 2
 
 CHUNKS = L * FG
 LAG = 2 * FG
+PASS_AHEAD = 2
+MOVE_AHEAD = 3
+RECON_LATE = 2
 
 FLOPS = 2 * T * D * F * (L + PAIRS)
 BYTES = (
@@ -36,18 +39,17 @@ def tile_crosslayertranscoder_e_kernel(
     tc, x, W_enc_words, W_enc_scales, b_enc, b_dec, W_dec_words, W_dec_scales, dec_mask, out
 ):
     nc = tc.nc
-    with tc.tile_pool(name="keep", bufs=1) as keep, tc.tile_pool(name="work", bufs=3) as work, tc.psum_pool(
-        name="psum_pre", bufs=2
-    ) as psum_pre, tc.psum_pool(name="psum_tr", bufs=2) as psum_tr, tc.psum_pool(
-        name="psum_acc", bufs=1
-    ) as psum_acc, tc.manual_schedule():
+    with tc.tile_pool(name="keep", bufs=1) as keep, tc.tile_pool(name="work", bufs=2) as work, tc.psum_pool(
+        name="psum_work", bufs=4
+    ) as psum_work, tc.psum_pool(name="psum_acc", bufs=1) as psum_acc, tc.manual_schedule():
         ident_f32 = keep.tile([P, P], F32)
         make_identity(nc, ident_f32[:])
 
+        enc_planes_raw = keep.tile([P, F], U8, align_bytes=64)
         enc_planes = keep.tile([P, F], U8, align_bytes=64)
         dec_planes = [keep.tile([P, (L - i) * FG, D], U8, name="dec_planes%d" % i, align_bytes=64) for i in range(L)]
         bias_rows = keep.tile([P, K_PASS], BF16)
-        nc.vector.memset(enc_planes[:].bitcast(I32), 0)
+        nc.vector.memset(enc_planes_raw[:].bitcast(I32), 0)
         nc.vector.memset(bias_rows[:], 0.0)
         for i in range(L):
             nc.vector.memset(dec_planes[i][:].rearrange("p s n -> p (s n)").bitcast(I32), 0)
@@ -58,15 +60,16 @@ def tile_crosslayertranscoder_e_kernel(
         nc.scalar.dma_start(out=bias_rows[CHUNKS : CHUNKS + L, :], in_=b_dec)
 
         x_sb = keep.tile([T, L, D], BF16)
-        for l in range(L):
-            nc.sync.dma_start(out=x_sb[:, l, :], in_=x[l])
+        enc_words = keep.tile([P, L, F], I32, align_bytes=64)
+        nc.sync.dma_start(out=x_sb[:, 0, :], in_=x[0])
         for quadrant in range(QUADRANTS):
             nc.sync.dma_start(
-                out=enc_planes[32 * quadrant : 32 * quadrant + 4 * L, :].bitcast(I32),
+                out=enc_planes_raw[32 * quadrant : 32 * quadrant + 4 * L, :].bitcast(I32),
                 in_=W_enc_scales[:, 4 * quadrant : 4 * quadrant + 4, :].bitcast(I32),
             )
-        enc_words = keep.tile([P, L, F], I32, align_bytes=64)
-        for l in range(L):
+        nc.sync.dma_start(out=enc_words[:, 0, :], in_=W_enc_words[0].rearrange("p n t -> p (n t)").bitcast(I32))
+        nc.sync.dma_start(out=x_sb[:, 1:L, :], in_=x[1:L].rearrange("l k d -> k l d"))
+        for l in range(1, L):
             nc.sync.dma_start(out=enc_words[:, l, :], in_=W_enc_words[l].rearrange("p n t -> p (n t)").bitcast(I32))
         dec_words = keep.tile([P, PAIRS * FG, D], I32, align_bytes=64)
         for i in range(L):
@@ -87,18 +90,28 @@ def tile_crosslayertranscoder_e_kernel(
         x_grouped = keep.tile([P, L, T * PACK], BF16, align_bytes=64)
         x_codes = keep.tile([P, L, T], I32, align_bytes=64)
         x_planes = keep.tile([P, L, T], U8, align_bytes=64)
-        for l in range(L):
+
+        def x_turn(l):
             x_pairs = x_sb[:, l, :].bitcast(F32)
-            xT = psum_tr.tile([P, 2, T], F32, tag="tr")
+            xT = psum_work.tile([P, 2, T], F32, tag="bank")
             for u in range(2):
                 nc.tensor.transpose(xT[:, u, :], x_pairs[:, u : D // 2 : 2], ident_f32[:])
             nc.scalar.copy(
                 out=x_grouped[:, l, :].bitcast(F32).rearrange("p (k u) -> p k u", u=2),
                 in_=xT[:].rearrange("p u k -> p k u"),
             )
+
+        def x_quantise(l):
             nc.vector.quantize_mx(out=x_codes[:, l, :].bitcast(FP8X4), scales=x_planes[:, l, :], in_=x_grouped[:, l, :])
 
-        biasT = psum_tr.tile([P, PACK, P], BF16, tag="tr")
+        x_turn(0)
+        nc.vector.tensor_copy(
+            out=enc_planes[:].rearrange("p (g t m) -> p g t m", t=PACK, m=P),
+            in_=enc_planes_raw[:].rearrange("p (g m t) -> p g t m", t=PACK, m=P),
+        )
+        x_quantise(0)
+
+        biasT = psum_work.tile([P, PACK, P], BF16, tag="bank")
         for t in range(PACK):
             nc.tensor.transpose(biasT[:, t, :], bias_rows[:, t:K_PASS:PACK], ident_bf16[:])
         enc_bias = keep.tile([P, CHUNKS, PACK], F32)
@@ -106,42 +119,45 @@ def tile_crosslayertranscoder_e_kernel(
 
         dec_bias = keep.tile([T, L, D], F32)
         for j in range(L):
-            spread = psum_pre.tile([T, D], F32, tag="pre")
+            spread = psum_work.tile([T, D], F32, tag="bank")
             row = CHUNKS + j
             nc.tensor.matmul(
                 out=spread[:], lhsT=ident_bf16[:, row : row + 1].to_broadcast([P, T]), rhs=bias_rows[:], start=True, stop=True
             )
             nc.scalar.copy(out=dec_bias[:, j, :], in_=spread[:])
 
+        enc_moved = keep.tile([P, CHUNKS, K_PASS], I32, align_bytes=64)
         acts_grouped = keep.tile([P, CHUNKS, T * PACK], BF16, align_bytes=64)
         acts_codes = keep.tile([P, CHUNKS, T], I32, align_bytes=64)
         acts_planes = keep.tile([P, CHUNKS, T], U8, align_bytes=64)
-        sorted_sums = {}
+        sums = {}
+
+        def encoder_move(chunk):
+            l, g = divmod(chunk, FG)
+            nc.vector.tensor_copy(
+                out=enc_moved[:, chunk, :].rearrange("p (t m) -> p t m", t=PACK),
+                in_=enc_words[:, l, g * K_PASS : (g + 1) * K_PASS].rearrange("p (m t) -> p t m", t=PACK),
+            )
 
         def encoder_pass(chunk):
             l, g = divmod(chunk, FG)
-            features = slice(g * K_PASS, (g + 1) * K_PASS)
-            pre = psum_pre.tile([T, K_PASS], F32, tag="pre")
-            nc.tensor.matmul_mx(
-                out=pre[:],
-                lhsT=x_codes[:, l, :].bitcast(FP8X4),
-                lhsT_scale=x_planes[:, l, :],
-                rhs=enc_words[:, l, features].bitcast(FP8X4),
-                rhs_scale=enc_planes[4 * l : P, features],
-                start=True,
-                stop=True,
-            )
-            pre_sorted = work.tile([T, PACK, P], F32)
-            nc.scalar.copy(out=pre_sorted[:], in_=pre[:].rearrange("k (p t) -> k t p", t=PACK))
-            sorted_sums[chunk] = pre_sorted
-
-        def encoder_transpose(chunk):
-            preT = psum_tr.tile([P, PACK, T], F32, tag="tr")
+            pre = psum_work.tile([P, PACK, T], F32, tag="bank")
             for t in range(PACK):
-                nc.tensor.transpose(preT[:, t, :], sorted_sums[chunk][:, t, :], ident_f32[:])
+                nc.tensor.matmul_mx(
+                    out=pre[:, t, :],
+                    lhsT=enc_moved[:, chunk, t * P : (t + 1) * P].bitcast(FP8X4),
+                    lhsT_scale=enc_planes[4 * l : P, g * K_PASS + t * P : g * K_PASS + (t + 1) * P],
+                    rhs=x_codes[:, l, :].bitcast(FP8X4),
+                    rhs_scale=x_planes[:, l, :],
+                    start=True,
+                    stop=True,
+                )
+            sums[chunk] = pre
+
+        def encoder_add(chunk):
             nc.vector.tensor_tensor(
                 out=acts_grouped[:, chunk, :].rearrange("p (k t) -> p k t", t=PACK),
-                in0=preT[:].rearrange("p t k -> p k t"),
+                in0=sums[chunk][:].rearrange("p t k -> p k t"),
                 in1=enc_bias[:, chunk, :].unsqueeze(1).to_broadcast([P, T, PACK]),
                 op=ADD,
             )
@@ -168,21 +184,38 @@ def tile_crosslayertranscoder_e_kernel(
                     start=(i == 0 and g == 0),
                     stop=(i == j and g == FG - 1),
                 )
-            if i == j:
-                recon = work.tile([T, D], F32)
-                nc.vector.tensor_tensor(out=recon[:], in0=acc[j][:], in1=dec_bias[:, j, :], op=ADD)
-                nc.sync.dma_start(out=out[j], in_=recon[:])
+
+        def decoder_store(j):
+            recon = work.tile([T, D], F32)
+            nc.vector.tensor_tensor(out=recon[:], in0=acc[j][:], in1=dec_bias[:, j, :], op=ADD)
+            nc.sync.dma_start(out=out[j], in_=recon[:])
 
         blocks = [(i, j) for i in range(L) for j in range(i, L)]
-        encoder_pass(0)
-        for step in range(LAG + PAIRS):
-            if step + 1 < CHUNKS:
-                encoder_pass(step + 1)
+        last_step = LAG + PAIRS - 1
+        for chunk in range(MOVE_AHEAD):
+            encoder_move(chunk)
+        for chunk in range(PASS_AHEAD):
+            encoder_pass(chunk)
+        for l in range(1, L):
+            x_turn(l)
+        store_at = {}
+        for step in range(last_step + 1):
+            if step + PASS_AHEAD < CHUNKS:
+                encoder_pass(step + PASS_AHEAD)
             if step >= LAG:
-                decoder_block(*blocks[step - LAG])
-            if 1 <= step <= CHUNKS:
-                encoder_relu(step - 1)
+                i, j = blocks[step - LAG]
+                decoder_block(i, j)
+                if i == j:
+                    store_at[min(step + RECON_LATE, last_step)] = store_at.get(min(step + RECON_LATE, last_step), []) + [j]
             if step < CHUNKS:
-                encoder_transpose(step)
+                encoder_add(step)
             if 1 <= step <= CHUNKS:
                 encoder_quantise(step - 1)
+            if step < CHUNKS:
+                encoder_relu(step)
+            if step + 1 < L:
+                x_quantise(step + 1)
+            if step + MOVE_AHEAD < CHUNKS:
+                encoder_move(step + MOVE_AHEAD)
+            for j in store_at.get(step, []):
+                decoder_store(j)

@@ -69,23 +69,39 @@ def tile_crosslayertranscoder_e_kernel(
             )
         nc.sync.dma_start(out=enc_words[:, 0, :], in_=W_enc_words[0].rearrange("p n t -> p (n t)").bitcast(I32))
         nc.sync.dma_start(out=x_sb[:, 1:L, :], in_=x[1:L].rearrange("l k d -> k l d"))
-        for l in range(1, L):
-            nc.sync.dma_start(out=enc_words[:, l, :], in_=W_enc_words[l].rearrange("p n t -> p (n t)").bitcast(I32))
         dec_words = keep.tile([P, PAIRS * FG, D], I32, align_bytes=64)
-        for i in range(L):
-            slot = first_slot(i)
-            group = (L * i + i) * FG
-            count = (L - i) * FG
-            for r in range(4):
-                nc.gpsimd.dma_start(
-                    out=dec_planes[i][4 * i + r : P : 32, :, :].bitcast(F32),
-                    in_=W_dec_scales[group : group + count, r : 16 : 4, :].rearrange("s q n -> q s n").bitcast(F32),
-                )
-            for at in range(0, count, FG):
-                nc.sync.dma_start(
-                    out=dec_words[:, slot + at : slot + at + FG, :],
-                    in_=W_dec_words[group + at : group + at + FG].rearrange("g p n t -> p g (n t)").bitcast(I32),
-                )
+
+        def first_group(i):
+            return (L * i + i) * FG
+
+        def load_enc_words(l):
+            nc.sync.dma_start(out=enc_words[:, l, :], in_=W_enc_words[l].rearrange("p n t -> p (n t)").bitcast(I32))
+
+        def load_dec_words(i, j):
+            slot = first_slot(i) + (j - i) * FG
+            group = first_group(i) + (j - i) * FG
+            nc.sync.dma_start(
+                out=dec_words[:, slot : slot + FG, :],
+                in_=W_dec_words[group : group + FG].rearrange("g p n t -> p g (n t)").bitcast(I32),
+            )
+
+        def load_dec_scales(i, r):
+            group = first_group(i)
+            nc.sync.dma_start(
+                out=dec_planes[i][4 * i + r : P : 32, :, :].bitcast(I32),
+                in_=W_dec_scales[group : group + (L - i) * FG, r : 16 : 4, :].rearrange("s q n -> q s n").bitcast(I32),
+            )
+
+        large = [(load_enc_words, (l,)) for l in range(1, L)] + [
+            (load_dec_words, (i, j)) for i in range(L) for j in range(i, L)
+        ]
+        small = [(i, r) for i in range(L) for r in range(4)]
+        for at, (load, which) in enumerate(large):
+            for pair in small[:2] if at < 4 else small[:1]:
+                load_dec_scales(*pair)
+                small.remove(pair)
+            load(*which)
+        assert not small
 
         x_grouped = keep.tile([P, L, T * PACK], BF16, align_bytes=64)
         x_codes = keep.tile([P, L, T], I32, align_bytes=64)

@@ -20,6 +20,7 @@ CHUNKS = L * FG
 LAG = 2 * FG
 PASS_AHEAD = 2
 MOVE_AHEAD = 3
+DMA_ALIGN = 256
 RECON_LATE = 2
 
 FLOPS = 2 * T * D * F * (L + PAIRS)
@@ -45,10 +46,10 @@ def tile_crosslayertranscoder_e_kernel(
         ident_f32 = keep.tile([P, P], F32)
         make_identity(nc, ident_f32[:])
 
-        enc_planes_raw = keep.tile([P, F], U8, align_bytes=64)
+        enc_planes_raw = keep.tile([P, F], U8, align_bytes=DMA_ALIGN)
         enc_planes = keep.tile([P, F], U8, align_bytes=64)
-        dec_planes = [keep.tile([P, (L - i) * FG, D], U8, name="dec_planes%d" % i, align_bytes=64) for i in range(L)]
-        bias_rows = keep.tile([P, K_PASS], BF16)
+        dec_planes = [keep.tile([P, (L - i) * FG, D], U8, name="dec_planes%d" % i, align_bytes=DMA_ALIGN) for i in range(L)]
+        bias_rows = keep.tile([P, K_PASS], BF16, align_bytes=DMA_ALIGN)
         nc.vector.memset(enc_planes_raw[:].bitcast(I32), 0)
         nc.vector.memset(bias_rows[:], 0.0)
         for i in range(L):
@@ -59,8 +60,8 @@ def tile_crosslayertranscoder_e_kernel(
         nc.scalar.dma_start(out=bias_rows[0:CHUNKS, :], in_=b_enc.rearrange("l (g k) -> (l g) k", k=K_PASS))
         nc.scalar.dma_start(out=bias_rows[CHUNKS : CHUNKS + L, :], in_=b_dec)
 
-        x_sb = keep.tile([T, L, D], BF16)
-        enc_words = keep.tile([P, L, F], I32, align_bytes=64)
+        x_sb = keep.tile([T, L, D], BF16, align_bytes=DMA_ALIGN)
+        enc_words = keep.tile([P, L, F], I32, align_bytes=DMA_ALIGN)
         nc.sync.dma_start(out=x_sb[:, 0, :], in_=x[0])
         for quadrant in range(QUADRANTS):
             nc.sync.dma_start(
@@ -69,7 +70,7 @@ def tile_crosslayertranscoder_e_kernel(
             )
         nc.sync.dma_start(out=enc_words[:, 0, :], in_=W_enc_words[0].rearrange("p n t -> p (n t)").bitcast(I32))
         nc.sync.dma_start(out=x_sb[:, 1:L, :], in_=x[1:L].rearrange("l k d -> k l d"))
-        dec_words = keep.tile([P, PAIRS * FG, D], I32, align_bytes=64)
+        dec_words = keep.tile([P, PAIRS * FG, D], I32, align_bytes=DMA_ALIGN)
 
         def first_group(i):
             return (L * i + i) * FG
@@ -202,7 +203,7 @@ def tile_crosslayertranscoder_e_kernel(
                 )
 
         def decoder_store(j):
-            recon = work.tile([T, D], F32)
+            recon = work.tile([T, D], F32, align_bytes=DMA_ALIGN)
             nc.vector.tensor_tensor(out=recon[:], in0=acc[j][:], in1=dec_bias[:, j, :], op=ADD)
             nc.sync.dma_start(out=out[j], in_=recon[:])
 

@@ -36,12 +36,18 @@ def first_slot(i):
     return FG * (i * L - i * (i - 1) // 2)
 
 
+def column_parts(j):
+    if j < L - 1:
+        return [slice(0, D)]
+    return [slice(0, D // 2), slice(D // 2, D)]
+
+
 def tile_crosslayertranscoder_e_kernel(
     tc, x, W_enc_words, W_enc_scales, b_enc, b_dec, W_dec_words, W_dec_scales, dec_mask, out
 ):
     nc = tc.nc
     with tc.tile_pool(name="keep", bufs=1) as keep, tc.tile_pool(name="work", bufs=2) as work, tc.psum_pool(
-        name="psum_work", bufs=4
+        name="psum_work", bufs=3
     ) as psum_work, tc.psum_pool(name="psum_acc", bufs=1) as psum_acc, tc.manual_schedule():
         ident_f32 = keep.tile([P, P], F32)
         make_identity(nc, ident_f32[:])
@@ -86,6 +92,12 @@ def tile_crosslayertranscoder_e_kernel(
                 in_=W_dec_words[group : group + FG].rearrange("g p n t -> p g (n t)").bitcast(I32),
             )
 
+        def load_dec_columns(i, j, g, columns):
+            nc.sync.dma_start(
+                out=dec_words[:, first_slot(i) + (j - i) * FG + g, columns],
+                in_=W_dec_words[first_group(i) + (j - i) * FG + g, :, columns, :].rearrange("p n t -> p (n t)").bitcast(I32),
+            )
+
         def load_dec_scales(i, r):
             group = first_group(i)
             nc.sync.dma_start(
@@ -94,7 +106,7 @@ def tile_crosslayertranscoder_e_kernel(
             )
 
         large = [(load_enc_words, (l,)) for l in range(1, L)] + [
-            (load_dec_words, (i, j)) for i in range(L) for j in range(i, L)
+            (load_dec_words, (i, j)) for i in range(L) for j in range(i, L) if i < L - 1
         ]
         small = [(i, r) for i in range(L) for r in range(4)]
         for at, (load, which) in enumerate(large):
@@ -103,6 +115,10 @@ def tile_crosslayertranscoder_e_kernel(
                 small.remove(pair)
             load(*which)
         assert not small
+        for g in range(FG - 1):
+            load_dec_columns(L - 1, L - 1, g, slice(0, D))
+        for columns in column_parts(L - 1):
+            load_dec_columns(L - 1, L - 1, FG - 1, columns)
 
         x_grouped = keep.tile([P, L, T * PACK], BF16, align_bytes=64)
         x_codes = keep.tile([P, L, T], I32, align_bytes=64)
@@ -187,25 +203,32 @@ def tile_crosslayertranscoder_e_kernel(
                 out=acts_codes[:, chunk, :].bitcast(FP8X4), scales=acts_planes[:, chunk, :], in_=acts_grouped[:, chunk, :]
             )
 
-        acc = [psum_acc.tile([T, D], F32, name="acc%d" % j) for j in range(L)]
+        acc = [
+            [psum_acc.tile([T, D], F32, name="acc%d_%d" % (j, part)) for part in range(len(column_parts(j)))]
+            for j in range(L)
+        ]
 
         def decoder_block(i, j):
             for g in range(FG):
                 at = (j - i) * FG + g
-                nc.tensor.matmul_mx(
-                    out=acc[j][:],
-                    lhsT=acts_codes[:, i * FG + g, :].bitcast(FP8X4),
-                    lhsT_scale=acts_planes[:, i * FG + g, :],
-                    rhs=dec_words[:, first_slot(i) + at, :].bitcast(FP8X4),
-                    rhs_scale=dec_planes[i][4 * i : P, at, :],
-                    start=(i == 0 and g == 0),
-                    stop=(i == j and g == FG - 1),
-                )
+                for part, columns in enumerate(column_parts(j)):
+                    nc.tensor.matmul_mx(
+                        out=acc[j][part][:, columns],
+                        lhsT=acts_codes[:, i * FG + g, :].bitcast(FP8X4),
+                        lhsT_scale=acts_planes[:, i * FG + g, :],
+                        rhs=dec_words[:, first_slot(i) + at, columns].bitcast(FP8X4),
+                        rhs_scale=dec_planes[i][4 * i : P, at, columns],
+                        start=(i == 0 and g == 0),
+                        stop=(i == j and g == FG - 1),
+                    )
 
         def decoder_store(j):
             recon = work.tile([T, D], F32, align_bytes=DMA_ALIGN)
-            nc.vector.tensor_tensor(out=recon[:], in0=acc[j][:], in1=dec_bias[:, j, :], op=ADD)
-            nc.sync.dma_start(out=out[j], in_=recon[:])
+            for part, columns in enumerate(column_parts(j)):
+                nc.vector.tensor_tensor(
+                    out=recon[:, columns], in0=acc[j][part][:, columns], in1=dec_bias[:, j, columns], op=ADD
+                )
+                nc.sync.dma_start(out=out[j, :, columns], in_=recon[:, columns])
 
         blocks = [(i, j) for i in range(L) for j in range(i, L)]
         last_step = LAG + PAIRS - 1

@@ -223,7 +223,7 @@ def tile_crosslayertranscoder_e_kernel(
                     )
 
         def decoder_store(j):
-            recon = work.tile([T, D], F32, align_bytes=DMA_ALIGN)
+            recon = work.tile([T, D], F32, bufs=L, align_bytes=DMA_ALIGN)
             for part, columns in enumerate(column_parts(j)):
                 nc.vector.tensor_tensor(
                     out=recon[:, columns], in0=acc[j][part][:, columns], in1=dec_bias[:, j, columns], op=ADD

import concourse.mybir as mybir
from concourse.masks import make_identity

F32 = mybir.dt.float32
BF16 = mybir.dt.bfloat16
I32 = mybir.dt.int32
U8 = mybir.dt.uint8
FP8X4 = mybir.dt.float8_e4m3fn_x4
ADD = mybir.AluOpType.add

L, T, F, D = 4, 128, 1536, 512
P = 128
PACK = 4
K_PASS = P * PACK
FG = F // K_PASS
QUADRANTS = 4
PAIRS = L * (L + 1) // 2

CHUNKS = L * FG
LAG = 2 * FG
PASS_AHEAD = 2
MOVE_AHEAD = 3
DMA_ALIGN = 256
RECON_LATE = 2

FLOPS = 2 * T * D * F * (L + PAIRS)
BYTES = (
    2 * L * T * D
    + (L + PAIRS) * (F * D + F * D // 32)
    + 2 * L * (F + D)
    + 4 * L * T * D
)


def first_slot(i):
    return FG * (i * L - i * (i - 1) // 2)


def column_parts(j):
    if j < L - 1:
        return [slice(0, D)]
    return [slice(0, D // 2), slice(D // 2, D)]


def tile_crosslayertranscoder_e_kernel(
    tc, x, W_enc_words, W_enc_scales, b_enc, b_dec, W_dec_words, W_dec_scales, dec_mask, out
):
    nc = tc.nc
    with tc.tile_pool(name="keep", bufs=1) as keep, tc.tile_pool(name="work", bufs=2) as work, tc.psum_pool(
        name="psum_work", bufs=3
    ) as psum_work, tc.psum_pool(name="psum_acc", bufs=1) as psum_acc, tc.manual_schedule():
        ident_f32 = keep.tile([P, P], F32)
        make_identity(nc, ident_f32[:])

        enc_planes_raw = keep.tile([P, F], U8, align_bytes=DMA_ALIGN)
        enc_planes = keep.tile([P, F], U8, align_bytes=64)
        dec_planes = [keep.tile([P, (L - i) * FG, D], U8, name="dec_planes%d" % i, align_bytes=DMA_ALIGN) for i in range(L)]
        bias_rows = keep.tile([P, K_PASS], BF16, align_bytes=DMA_ALIGN)
        nc.vector.memset(enc_planes_raw[:].bitcast(I32), 0)
        nc.vector.memset(bias_rows[:], 0.0)
        for i in range(L):
            nc.vector.memset(dec_planes[i][:].rearrange("p s n -> p (s n)").bitcast(I32), 0)
        ident_bf16 = keep.tile([P, P], BF16)
        nc.vector.tensor_copy(out=ident_bf16[:], in_=ident_f32[:])

        nc.scalar.dma_start(out=bias_rows[0:CHUNKS, :], in_=b_enc.rearrange("l (g k) -> (l g) k", k=K_PASS))
        nc.scalar.dma_start(out=bias_rows[CHUNKS : CHUNKS + L, :], in_=b_dec)

        x_sb = keep.tile([T, L, D], BF16, align_bytes=DMA_ALIGN)
        enc_words = keep.tile([P, L, F], I32, align_bytes=DMA_ALIGN)
        nc.sync.dma_start(out=x_sb[:, 0, :], in_=x[0])
        for quadrant in range(QUADRANTS):
            nc.sync.dma_start(
                out=enc_planes_raw[32 * quadrant : 32 * quadrant + 4 * L, :].bitcast(I32),
                in_=W_enc_scales[:, 4 * quadrant : 4 * quadrant + 4, :].bitcast(I32),
            )
        nc.sync.dma_start(out=enc_words[:, 0, :], in_=W_enc_words[0].rearrange("p n t -> p (n t)").bitcast(I32))
        nc.sync.dma_start(out=x_sb[:, 1:L, :], in_=x[1:L].rearrange("l k d -> k l d"))
        dec_words = keep.tile([P, PAIRS * FG, D], I32, align_bytes=DMA_ALIGN)

        def first_group(i):
            return (L * i + i) * FG

        def load_enc_words(l):
            nc.sync.dma_start(out=enc_words[:, l, :], in_=W_enc_words[l].rearrange("p n t -> p (n t)").bitcast(I32))

        def load_dec_words(i, j):
            slot = first_slot(i) + (j - i) * FG
            group = first_group(i) + (j - i) * FG
            nc.sync.dma_start(
                out=dec_words[:, slot : slot + FG, :],
                in_=W_dec_words[group : group + FG].rearrange("g p n t -> p g (n t)").bitcast(I32),
            )

        def load_dec_columns(i, j, g, columns):
            nc.sync.dma_start(
                out=dec_words[:, first_slot(i) + (j - i) * FG + g, columns],
                in_=W_dec_words[first_group(i) + (j - i) * FG + g, :, columns, :].rearrange("p n t -> p (n t)").bitcast(I32),
            )

        def load_dec_scales(i, r):
            group = first_group(i)
            nc.sync.dma_start(
                out=dec_planes[i][4 * i + r : P : 32, :, :].bitcast(I32),
                in_=W_dec_scales[group : group + (L - i) * FG, r : 16 : 4, :].rearrange("s q n -> q s n").bitcast(I32),
            )

        large = [(load_enc_words, (l,)) for l in range(1, L)] + [
            (load_dec_words, (i, j)) for i in range(L) for j in range(i, L) if i < L - 1
        ]
        small = [(i, r) for i in range(L) for r in range(4)]
        for at, (load, which) in enumerate(large):
            for pair in small[:2] if at < 4 else small[:1]:
                load_dec_scales(*pair)
                small.remove(pair)
            load(*which)
        assert not small
        for g in range(FG - 1):
            load_dec_columns(L - 1, L - 1, g, slice(0, D))
        for columns in column_parts(L - 1):
            load_dec_columns(L - 1, L - 1, FG - 1, columns)

        x_grouped = keep.tile([P, L, T * PACK], BF16, align_bytes=64)
        x_codes = keep.tile([P, L, T], I32, align_bytes=64)
        x_planes = keep.tile([P, L, T], U8, align_bytes=64)

        def x_turn(l):
            x_pairs = x_sb[:, l, :].bitcast(F32)
            xT = psum_work.tile([P, 2, T], F32, tag="bank")
            for u in range(2):
                nc.tensor.transpose(xT[:, u, :], x_pairs[:, u : D // 2 : 2], ident_f32[:])
            nc.scalar.copy(
                out=x_grouped[:, l, :].bitcast(F32).rearrange("p (k u) -> p k u", u=2),
                in_=xT[:].rearrange("p u k -> p k u"),
            )

        def x_quantise(l):
            nc.vector.quantize_mx(out=x_codes[:, l, :].bitcast(FP8X4), scales=x_planes[:, l, :], in_=x_grouped[:, l, :])

        x_turn(0)
        nc.vector.tensor_copy(
            out=enc_planes[:].rearrange("p (g t m) -> p g t m", t=PACK, m=P),
            in_=enc_planes_raw[:].rearrange("p (g m t) -> p g t m", t=PACK, m=P),
        )
        x_quantise(0)

        biasT = psum_work.tile([P, PACK, P], BF16, tag="bank")
        for t in range(PACK):
            nc.tensor.transpose(biasT[:, t, :], bias_rows[:, t:K_PASS:PACK], ident_bf16[:])
        enc_bias = keep.tile([P, CHUNKS, PACK], F32)
        nc.vector.tensor_copy(out=enc_bias[:], in_=biasT[:, :, 0:CHUNKS].rearrange("p t r -> p r t"))

        dec_bias = keep.tile([T, L, D], F32)
        for j in range(L):
            spread = psum_work.tile([T, D], F32, tag="bank")
            row = CHUNKS + j
            nc.tensor.matmul(
                out=spread[:], lhsT=ident_bf16[:, row : row + 1].to_broadcast([P, T]), rhs=bias_rows[:], start=True, stop=True
            )
            nc.scalar.copy(out=dec_bias[:, j, :], in_=spread[:])

        enc_moved = keep.tile([P, CHUNKS, K_PASS], I32, align_bytes=64)
        acts_grouped = keep.tile([P, CHUNKS, T * PACK], BF16, align_bytes=64)
        acts_codes = keep.tile([P, CHUNKS, T], I32, align_bytes=64)
        acts_planes = keep.tile([P, CHUNKS, T], U8, align_bytes=64)
        sums = {}

        def encoder_move(chunk):
            l, g = divmod(chunk, FG)
            nc.vector.tensor_copy(
                out=enc_moved[:, chunk, :].rearrange("p (t m) -> p t m", t=PACK),
                in_=enc_words[:, l, g * K_PASS : (g + 1) * K_PASS].rearrange("p (m t) -> p t m", t=PACK),
            )

        def encoder_pass(chunk):
            l, g = divmod(chunk, FG)
            pre = psum_work.tile([P, PACK, T], F32, tag="bank")
            for t in range(PACK):
                nc.tensor.matmul_mx(
                    out=pre[:, t, :],
                    lhsT=enc_moved[:, chunk, t * P : (t + 1) * P].bitcast(FP8X4),
                    lhsT_scale=enc_planes[4 * l : P, g * K_PASS + t * P : g * K_PASS + (t + 1) * P],
                    rhs=x_codes[:, l, :].bitcast(FP8X4),
                    rhs_scale=x_planes[:, l, :],
                    start=True,
                    stop=True,
                )
            sums[chunk] = pre

        def encoder_add(chunk):
            nc.vector.tensor_tensor(
                out=acts_grouped[:, chunk, :].rearrange("p (k t) -> p k t", t=PACK),
                in0=sums[chunk][:].rearrange("p t k -> p k t"),
                in1=enc_bias[:, chunk, :].unsqueeze(1).to_broadcast([P, T, PACK]),
                op=ADD,
            )

        def encoder_relu(chunk):
            nc.vector.tensor_scalar_max(out=acts_grouped[:, chunk, :], in0=acts_grouped[:, chunk, :], scalar1=0.0)

        def encoder_quantise(chunk):
            nc.vector.quantize_mx(
                out=acts_codes[:, chunk, :].bitcast(FP8X4), scales=acts_planes[:, chunk, :], in_=acts_grouped[:, chunk, :]
            )

        acc = [
            [psum_acc.tile([T, D], F32, name="acc%d_%d" % (j, part)) for part in range(len(column_parts(j)))]
            for j in range(L)
        ]

        def decoder_block(i, j):
            for g in range(FG):
                at = (j - i) * FG + g
                for part, columns in enumerate(column_parts(j)):
                    nc.tensor.matmul_mx(
                        out=acc[j][part][:, columns],
                        lhsT=acts_codes[:, i * FG + g, :].bitcast(FP8X4),
                        lhsT_scale=acts_planes[:, i * FG + g, :],
                        rhs=dec_words[:, first_slot(i) + at, columns].bitcast(FP8X4),
                        rhs_scale=dec_planes[i][4 * i : P, at, columns],
                        start=(i == 0 and g == 0),
                        stop=(i == j and g == FG - 1),
                    )

        def decoder_store(j):
            recon = work.tile([T, D], F32, bufs=L, align_bytes=DMA_ALIGN)
            for part, columns in enumerate(column_parts(j)):
                nc.vector.tensor_tensor(
                    out=recon[:, columns], in0=acc[j][part][:, columns], in1=dec_bias[:, j, columns], op=ADD
                )
                nc.sync.dma_start(out=out[j, :, columns], in_=recon[:, columns])

        blocks = [(i, j) for i in range(L) for j in range(i, L)]
        last_step = LAG + PAIRS - 1
        for chunk in range(MOVE_AHEAD):
            encoder_move(chunk)
        for chunk in range(PASS_AHEAD):
            encoder_pass(chunk)
        for l in range(1, L):
            x_turn(l)
        store_at = {}
        for step in range(last_step + 1):
            if step + PASS_AHEAD < CHUNKS:
                encoder_pass(step + PASS_AHEAD)
            if step >= LAG:
                i, j = blocks[step - LAG]
                decoder_block(i, j)
                if i == j:
                    store_at[min(step + RECON_LATE, last_step)] = store_at.get(min(step + RECON_LATE, last_step), []) + [j]
            if step < CHUNKS:
                encoder_add(step)
            if 1 <= step <= CHUNKS:
                encoder_quantise(step - 1)
            if step < CHUNKS:
                encoder_relu(step)
            if step + 1 < L:
                x_quantise(step + 1)
            if step + MOVE_AHEAD < CHUNKS:
                encoder_move(step + MOVE_AHEAD)
            for j in store_at.get(step, []):
                decoder_store(j)
